import numpy as np
import ml_dtypes


def mxq(x, axis, fmt="e4m3"):
    dtype, down = {"e4m3": (ml_dtypes.float8_e4m3fn, 7), "e5m2": (ml_dtypes.float8_e5m2, 14)}[fmt]
    v = np.moveaxis(np.asarray(x, np.float32).astype(ml_dtypes.bfloat16).astype(np.float64), axis, -1)
    blocks = v.reshape(v.shape[:-1] + (-1, 32))
    amax = np.abs(blocks).max(-1, keepdims=True)
    byte = np.maximum(np.where(amax > 0, np.frexp(amax)[1] - 1 + 127, 0) - down, 1)
    scale = np.exp2(byte - 127.0)
    codes = (blocks / scale).astype(np.float32).astype(dtype).astype(np.float64)
    return np.moveaxis((codes * scale).reshape(v.shape), -1, axis)


WIDE = False


def mx_kscale(k):
    if not WIDE:
        return np.ones(k)
    levels = np.array([10, -10, 5, -5, 0])
    a = np.random.permutation(np.resize(levels, k // 512 * 4)).reshape(k // 512, 4)
    idx = np.arange(k)
    return np.exp2(a[idx // 512, idx % 128 // 32])


BF16 = ml_dtypes.bfloat16


def bf(x):
    return np.asarray(x, np.float32).astype(BF16)


def f64(x):
    return np.asarray(x).astype(np.float64)


NTR, NTE, D, C = 8192, 4096, 512, 128


def setup_inputs():
    s = mx_kscale(D)
    return {"x_train": bf(np.random.standard_normal((NTR, D)) * s),
            "x_test": bf(np.random.standard_normal((NTE, D)) * s),
            "M": bf(np.random.standard_normal((D, D)) / np.sqrt(D) / s[:, None] / s[None, :])}


def reference(x_train, x_test, M):
    xs, xc = f64(x_train), f64(x_test)
    Mq = mxq(f64(M), 0, "e4m3")
    sM = mxq(xs, 1, "e4m3") @ Mq
    s_norm2 = (sM * xs).sum(-1)
    c_norm2 = ((mxq(xc, 1, "e4m3") @ Mq) * xc).sum(-1)
    return (sM, s_norm2, c_norm2)

@@ -1,0 +1,180 @@
+from contextlib import ExitStack
+
+import concourse.mybir as mybir
+from concourse.masks import make_identity
+
+FP8X4 = mybir.dt.float8_e4m3fn_x4
+BF16 = mybir.dt.bfloat16
+F32 = mybir.dt.float32
+U32 = mybir.dt.uint32
+U8 = mybir.dt.uint8
+MULT = mybir.AluOpType.mult
+
+P = 128
+D = 512
+W = D // 2
+TRAIN_TILES = 64
+TEST_TILES = 32
+GT = 4
+SUPER = 8
+NG = 3 * SUPER
+
+FLOPS = 2 * (TRAIN_TILES + TEST_TILES) * P * D * D
+
+
+def tile_rbfnet_pa_t_kernel(tc, x_train, x_test, M, out_0, out_1, out_2):
+    nc = tc.nc
+    xtr_d = x_train.rearrange("(p t) k -> p (t k)", t=TRAIN_TILES)
+    xte_d = x_test.rearrange("(p t) k -> p (t k)", t=TEST_TILES)
+    sm_d = out_0.rearrange("(p t) k -> p (t k)", t=TRAIN_TILES)
+    sn_d = out_1.rearrange("(p t) -> p t", t=TRAIN_TILES)
+    cn_d = out_2.rearrange("(p t) -> p t", t=TEST_TILES)
+
+    with ExitStack() as ctx:
+        keep = ctx.enter_context(tc.tile_pool(name="keep", bufs=1))
+        grp_pool = ctx.enter_context(tc.tile_pool(name="grp", bufs=3))
+        q_pool = ctx.enter_context(tc.tile_pool(name="q", bufs=3))
+        sm_pool = ctx.enter_context(tc.tile_pool(name="smsb", bufs=8))
+        junk_pool = ctx.enter_context(tc.tile_pool(name="junk", bufs=2))
+        xt_pool = ctx.enter_context(tc.psum_pool(name="xtps", bufs=2))
+        ps_pool = ctx.enter_context(tc.psum_pool(name="smps", bufs=6))
+        ctx.enter_context(tc.manual_schedule())
+
+        groups = []
+
+        def load(src, t0, n, name):
+            xt = keep.tile([P, n * D], BF16, name=name)
+            nc.sync.dma_start(out=xt[:], in_=src[:, t0 * D : (t0 + n) * D])
+            return xt
+
+        m_raw = keep.tile([P, 4 * D], BF16, name="m_raw")
+        for s in range(SUPER):
+            if s == 0:
+                a = load(xtr_d, 0, GT, "xtr0a")
+                nc.sync.dma_start(
+                    out=m_raw[:].rearrange("p (u ec) -> p u ec", u=2),
+                    in_=M.rearrange("(u q e) c -> q u (e c)", u=2, e=2),
+                )
+                b = load(xtr_d, GT, GT, "xtr0b")
+                groups.append((True, 0, a, 0))
+                groups.append((True, GT, b, 0))
+            else:
+                a = load(xtr_d, 2 * GT * s, 2 * GT, "xtr%d" % s)
+                groups.append((True, 2 * GT * s, a, 0))
+                groups.append((True, 2 * GT * s + GT, a, GT * D))
+            c = load(xte_d, GT * s, GT, "xte%d" % s)
+            groups.append((False, GT * s, c, 0))
+
+        ident = keep.tile([P, P], F32, name="ident")
+        make_identity(nc, ident[:])
+
+        s_norm = keep.tile([P, TRAIN_TILES], F32, name="s_norm")
+        c_norm = keep.tile([P, TEST_TILES], F32, name="c_norm")
+
+        m_grp = keep.tile([P, 4 * D], BF16, name="m_grp", align_bytes=64)
+        m_codes = keep.tile([P, D], U32, name="m_codes", align_bytes=64)
+        m_scales = keep.tile([P, D], U8, name="m_scales", align_bytes=64)
+        nc.vector.tensor_copy(
+            out=m_grp[:].rearrange("p (c i t) -> p c t i", i=4, t=4),
+            in_=m_raw[:].rearrange("p (t c i) -> p c t i", t=4, i=4),
+        )
+        nc.vector.quantize_mx(out=m_codes[:].bitcast(FP8X4), scales=m_scales[:], in_=m_grp[:])
+
+        xt_tiles = {}
+        grp_tiles = {}
+        q_tiles = {}
+        ps_tiles = {}
+        sb_tiles = {}
+
+        def transposes(g):
+            x_f32 = groups[g][2][:].bitcast(F32)
+            off = groups[g][3] // 2
+            banks = []
+            for b in range(2):
+                xt = xt_pool.tile([P, 4 * P], F32, name="xt")
+                for a in range(2):
+                    for u in range(2):
+                        col = off + (2 * b + a) * W + u * P
+                        nc.tensor.transpose(
+                            xt[:, (2 * a + u) * P : (2 * a + u + 1) * P],
+                            x_f32[:, col : col + P],
+                            ident[:],
+                        )
+                banks.append(xt)
+            xt_tiles[g] = banks
+
+        def copy_out(g):
+            grp = grp_pool.tile([P, GT * P * 4], BF16, name="grp", align_bytes=64)
+            g_f32 = grp[:].bitcast(F32)
+            for b in range(2):
+                nc.scalar.copy(
+                    out=g_f32[:, 4 * P * b : 4 * P * (b + 1)].rearrange(
+                        "p (a r u) -> p a r u", a=2, u=2
+                    ),
+                    in_=xt_tiles[g][b][:].rearrange("p (a u r) -> p a r u", a=2, u=2),
+                )
+            grp_tiles[g] = grp
+
+        def quantise(g):
+            codes = q_pool.tile([P, GT * P], U32, name="codes", align_bytes=64)
+            scales = q_pool.tile([P, GT * P], U8, name="scales", align_bytes=64)
+            nc.vector.quantize_mx(
+                out=codes[:].bitcast(FP8X4), scales=scales[:], in_=grp_tiles[g][:]
+            )
+            q_tiles[g] = (codes, scales)
+
+        def mx(g, i):
+            codes, scales = q_tiles[g]
+            acc = ps_pool.tile([P, D], F32, name="acc")
+            nc.tensor.matmul_mx(
+                out=acc[:],
+                lhsT=codes[:, i * P : (i + 1) * P].bitcast(FP8X4),
+                lhsT_scale=scales[:, i * P : (i + 1) * P],
+                rhs=m_codes[:].bitcast(FP8X4),
+                rhs_scale=m_scales[:],
+                start=True,
+                stop=True,
+            )
+            ps_tiles[(g, i)] = acc
+
+        def finish(g, i):
+            is_train, t0, xtile, off = groups[g]
+            acc = ps_tiles[(g, i)]
+            x_in = xtile[:, off + i * D : off + (i + 1) * D]
+            if is_train:
+                if i == 0:
+                    sb_tiles[g] = sm_pool.tile([P, GT * D], F32, name="sm_sb")
+                dst = sb_tiles[g][:, i * D : (i + 1) * D]
+                nc.vector.scalar_tensor_tensor(
+                    out=dst, in0=acc[:], scalar=1.0, in1=x_in, op0=MULT, op1=MULT,
+                    accum_out=s_norm[:, t0 + i : t0 + i + 1],
+                )
+                nc.scalar.copy(out=dst, in_=acc[:])
+            else:
+                junk = junk_pool.tile([P, D], F32, name="junk")
+                nc.vector.scalar_tensor_tensor(
+                    out=junk[:], in0=acc[:], scalar=1.0, in1=x_in, op0=MULT, op1=MULT,
+                    accum_out=c_norm[:, t0 + i : t0 + i + 1],
+                )
+
+        for j in range(-3, NG):
+            if 0 <= j + 2 < NG:
+                copy_out(j + 2)
+            if 0 <= j + 3 < NG:
+                transposes(j + 3)
+            has_next = 0 <= j + 1 < NG
+            if has_next:
+                quantise(j + 1)
+                mx(j + 1, 0)
+                mx(j + 1, 1)
+            for i in range(GT):
+                if j >= 0:
+                    finish(j, i)
+                if has_next and i < 2:
+                    mx(j + 1, i + 2)
+            if j >= 0 and groups[j][0]:
+                t0 = groups[j][1]
+                nc.sync.dma_start(out=sm_d[:, t0 * D : (t0 + GT) * D], in_=sb_tiles[j][:])
+            if j == NG - 2:
+                nc.sync.dma_start(out=sn_d, in_=s_norm[:])
+        nc.sync.dma_start(out=cn_d, in_=c_norm[:])

@@ -9,6 +9,7 @@ F32 = mybir.dt.float32
 U32 = mybir.dt.uint32
 U8 = mybir.dt.uint8
 MULT = mybir.AluOpType.mult
+ADD = mybir.AluOpType.add
 
 P = 128
 D = 512
@@ -18,8 +19,33 @@ TEST_TILES = 32
 GT = 4
 SUPER = 8
 NG = 3 * SUPER
+G_TILES = [2, 2, 2, 2, 2, 2, 2, 0]
+G_MAX = 3
+R_LAG = 5
+FOLD = 64
 
 FLOPS = 2 * (TRAIN_TILES + TEST_TILES) * P * D * D
+
+
+def make_sequence():
+    seq = []
+    for s in range(SUPER):
+        n = G_TILES[s]
+        rest = [8 * s] + [8 * s + 1 + n + i for i in range(7 - n)]
+        r = 0
+        e = 0
+        for gi in range(3):
+            n_tr = 3 if gi < 2 else 2
+            if gi < n:
+                seq.append((True, 8 * s + 1 + gi, True))
+                n_tr -= 1
+            for i in range(n_tr):
+                seq.append((True, rest[r], False))
+                r += 1
+            for i in range(GT - (3 if gi < 2 else 2)):
+                seq.append((False, 4 * s + e, False))
+                e += 1
+    return seq
 
 
 def tile_rbfnet_pa_t_kernel(tc, x_train, x_test, M, out_0, out_1, out_2):
@@ -29,6 +55,7 @@ def tile_rbfnet_pa_t_kernel(tc, x_train, x_test, M, out_0, out_1, out_2):
     sm_d = out_0.rearrange("(p t) k -> p (t k)", t=TRAIN_TILES)
     sn_d = out_1.rearrange("(p t) -> p t", t=TRAIN_TILES)
     cn_d = out_2.rearrange("(p t) -> p t", t=TEST_TILES)
+    seq = make_sequence()
 
     with ExitStack() as ctx:
         keep = ctx.enter_context(tc.tile_pool(name="keep", bufs=1))
@@ -40,13 +67,12 @@ def tile_rbfnet_pa_t_kernel(tc, x_train, x_test, M, out_0, out_1, out_2):
         ps_pool = ctx.enter_context(tc.psum_pool(name="smps", bufs=6))
         ctx.enter_context(tc.manual_schedule())
 
-        groups = []
-
         def load(src, t0, n, name):
             xt = keep.tile([P, n * D], BF16, name=name)
             nc.sync.dma_start(out=xt[:], in_=src[:, t0 * D : (t0 + n) * D])
             return xt
 
+        x_src = {}
         m_raw = keep.tile([P, 4 * D], BF16, name="m_raw")
         for s in range(SUPER):
             if s == 0:
@@ -55,21 +81,28 @@ def tile_rbfnet_pa_t_kernel(tc, x_train, x_test, M, out_0, out_1, out_2):
                     out=m_raw[:].rearrange("p (u ec) -> p u ec", u=2),
                     in_=M.rearrange("(u q e) c -> q u (e c)", u=2, e=2),
                 )
+                c = load(xte_d, 0, GT, "xte0")
                 b = load(xtr_d, GT, GT, "xtr0b")
-                groups.append((True, 0, a, 0))
-                groups.append((True, GT, b, 0))
+                for i in range(GT):
+                    x_src[(True, i)] = (a, i * D)
+                    x_src[(True, GT + i)] = (b, i * D)
             else:
                 a = load(xtr_d, 2 * GT * s, 2 * GT, "xtr%d" % s)
-                groups.append((True, 2 * GT * s, a, 0))
-                groups.append((True, 2 * GT * s + GT, a, GT * D))
-            c = load(xte_d, GT * s, GT, "xte%d" % s)
-            groups.append((False, GT * s, c, 0))
+                c = load(xte_d, GT * s, GT, "xte%d" % s)
+                for i in range(2 * GT):
+                    x_src[(True, 2 * GT * s + i)] = (a, i * D)
+            for i in range(GT):
+                x_src[(False, GT * s + i)] = (c, i * D)
 
         ident = keep.tile([P, P], F32, name="ident")
         make_identity(nc, ident[:])
 
         s_norm = keep.tile([P, TRAIN_TILES], F32, name="s_norm")
         c_norm = keep.tile([P, TEST_TILES], F32, name="c_norm")
+        g_part = keep.tile([P, SUPER * G_MAX * FOLD], F32, name="g_part")
+        g_prod = keep.tile([P, G_MAX * D], F32, name="g_prod")
+        g_f1 = keep.tile([P, G_MAX * D // 2], F32, name="g_f1")
+        g_f2 = keep.tile([P, G_MAX * D // 4], F32, name="g_f2")
 
         m_grp = keep.tile([P, 4 * D], BF16, name="m_grp", align_bytes=64)
         m_codes = keep.tile([P, D], U32, name="m_codes", align_bytes=64)
@@ -85,16 +118,19 @@ def tile_rbfnet_pa_t_kernel(tc, x_train, x_test, M, out_0, out_1, out_2):
         q_tiles = {}
         ps_tiles = {}
         sb_tiles = {}
+        copied = {}
+        g_copied = {}
 
         def transposes(g):
-            x_f32 = groups[g][2][:].bitcast(F32)
-            off = groups[g][3] // 2
             banks = []
             for b in range(2):
                 xt = xt_pool.tile([P, 4 * P], F32, name="xt")
                 for a in range(2):
+                    is_train, t, on_g = seq[GT * g + 2 * b + a]
+                    xtile, off = x_src[(is_train, t)]
+                    x_f32 = xtile[:].bitcast(F32)
                     for u in range(2):
-                        col = off + (2 * b + a) * W + u * P
+                        col = off // 2 + u * P
                         nc.tensor.transpose(
                             xt[:, (2 * a + u) * P : (2 * a + u + 1) * P],
                             x_f32[:, col : col + P],
@@ -137,25 +173,88 @@ def tile_rbfnet_pa_t_kernel(tc, x_train, x_test, M, out_0, out_1, out_2):
             )
             ps_tiles[(g, i)] = acc
 
+        def halves(ap, n, width):
+            v = ap[:, : n * width].rearrange("p (n w) -> p n w", n=n)
+            return v[:, :, : width // 2], v[:, :, width // 2 :]
+
+        def gpsimd_batch(s):
+            n = G_TILES[s]
+            t0 = 8 * s + 1
+            xtile, off = x_src[(True, t0)]
+            sb = sb_tiles[t0 // GT]
+            col = (t0 % GT) * D
+            nc.gpsimd.tensor_tensor(
+                out=g_prod[:, : n * D],
+                in0=sb[:, col : col + n * D],
+                in1=xtile[:, off : off + n * D],
+                op=MULT,
+            )
+            lo, hi = halves(g_prod, n, D)
+            nc.gpsimd.tensor_tensor(
+                out=g_f1[:, : n * D // 2].rearrange("p (n w) -> p n w", n=n), in0=lo, in1=hi, op=ADD
+            )
+            lo, hi = halves(g_f1, n, D // 2)
+            nc.gpsimd.tensor_tensor(
+                out=g_f2[:, : n * D // 4].rearrange("p (n w) -> p n w", n=n), in0=lo, in1=hi, op=ADD
+            )
+            lo, hi = halves(g_f2, n, D // 4)
+            base = s * G_MAX * FOLD
+            nc.gpsimd.tensor_tensor(
+                out=g_part[:, base : base + n * FOLD].rearrange("p (n w) -> p n w", n=n),
+                in0=lo, in1=hi, op=ADD,
+            )
+
+        def reduce_batch(s):
+            n = G_TILES[s]
+            base = s * G_MAX * FOLD
+            nc.vector.tensor_reduce(
+                out=s_norm[:, 8 * s + 1 : 8 * s + 1 + n],
+                in_=g_part[:, base : base + n * FOLD].rearrange("p (n w) -> p n w", n=n),
+                axis=mybir.AxisListType.X,
+                op=ADD,
+            )
+
         def finish(g, i):
-            is_train, t0, xtile, off = groups[g]
+            is_train, t, on_g = seq[GT * g + i]
+            xtile, off = x_src[(is_train, t)]
             acc = ps_tiles[(g, i)]
-            x_in = xtile[:, off + i * D : off + (i + 1) * D]
-            if is_train:
-                if i == 0:
-                    sb_tiles[g] = sm_pool.tile([P, GT * D], F32, name="sm_sb")
-                dst = sb_tiles[g][:, i * D : (i + 1) * D]
-                nc.vector.scalar_tensor_tensor(
-                    out=dst, in0=acc[:], scalar=1.0, in1=x_in, op0=MULT, op1=MULT,
-                    accum_out=s_norm[:, t0 + i : t0 + i + 1],
-                )
-                nc.scalar.copy(out=dst, in_=acc[:])
-            else:
+            x_in = xtile[:, off : off + D]
+            if not is_train:
                 junk = junk_pool.tile([P, D], F32, name="junk")
                 nc.vector.scalar_tensor_tensor(
                     out=junk[:], in0=acc[:], scalar=1.0, in1=x_in, op0=MULT, op1=MULT,
-                    accum_out=c_norm[:, t0 + i : t0 + i + 1],
+                    accum_out=c_norm[:, t : t + 1],
                 )
+                return
+            h = t // GT
+            if h not in sb_tiles:
+                sb_tiles[h] = sm_pool.tile([P, GT * D], F32, name="sm_sb")
+                copied[h] = 0
+            dst = sb_tiles[h][:, (t % GT) * D : (t % GT + 1) * D]
+            if not on_g:
+                nc.vector.scalar_tensor_tensor(
+                    out=dst, in0=acc[:], scalar=1.0, in1=x_in, op0=MULT, op1=MULT,
+                    accum_out=s_norm[:, t : t + 1],
+                )
+            nc.scalar.copy(out=dst, in_=acc[:])
+            copied[h] += 1
+            if on_g:
+                s = t // 8
+                g_copied[s] = g_copied.get(s, 0) + 1
+                if g_copied[s] == G_TILES[s]:
+                    gpsimd_batch(s)
+            if copied[h] == GT:
+                nc.sync.dma_start(out=sm_d[:, h * GT * D : (h + 1) * GT * D], in_=sb_tiles[h][:])
+
+        reduce_at = {}
+        late = []
+        for s in range(SUPER):
+            if G_TILES[s] > 0:
+                it = 3 * s + G_TILES[s] - 1 + R_LAG
+                if it < NG:
+                    reduce_at[it] = s
+                else:
+                    late.append(s)
 
         for j in range(-3, NG):
             if 0 <= j + 2 < NG:
@@ -167,14 +266,14 @@ def tile_rbfnet_pa_t_kernel(tc, x_train, x_test, M, out_0, out_1, out_2):
                 quantise(j + 1)
                 mx(j + 1, 0)
                 mx(j + 1, 1)
+            if j in reduce_at:
+                reduce_batch(reduce_at[j])
             for i in range(GT):
                 if j >= 0:
                     finish(j, i)
                 if has_next and i < 2:
                     mx(j + 1, i + 2)
-            if j >= 0 and groups[j][0]:
-                t0 = groups[j][1]
-                nc.sync.dma_start(out=sm_d[:, t0 * D : (t0 + GT) * D], in_=sb_tiles[j][:])
-            if j == NG - 2:
-                nc.sync.dma_start(out=sn_d, in_=s_norm[:])
         nc.sync.dma_start(out=cn_d, in_=c_norm[:])
+        for s in late:
+            reduce_batch(s)
+        nc.sync.dma_start(out=sn_d, in_=s_norm[:])

@@ -13,39 +13,37 @@ ADD = mybir.AluOpType.add
 
 P = 128
 D = 512
-W = D // 2
 TRAIN_TILES = 64
 TEST_TILES = 32
 GT = 4
-SUPER = 8
-NG = 3 * SUPER
-G_TILES = [2, 2, 2, 2, 2, 2, 2, 0]
-G_MAX = 3
-R_LAG = 5
+N_TRAIN_G = TRAIN_TILES // GT
+N_TEST_G = TEST_TILES // GT
+NL = N_TRAIN_G + N_TEST_G
+P1_TESTS = 24
+TAIL_TESTS = 2
+G_GROUPS = [0, 2, 4, 6, 8, 10, 12]
+G_N = 2
 FOLD = 64
+LOOK = 4
+R_EARLY = 5
+R_EARLY_AT = 14
 
 FLOPS = 2 * (TRAIN_TILES + TEST_TILES) * P * D * D
 
 
-def make_sequence():
-    seq = []
-    for s in range(SUPER):
-        n = G_TILES[s]
-        rest = [8 * s] + [8 * s + 1 + n + i for i in range(7 - n)]
-        r = 0
-        e = 0
-        for gi in range(3):
-            n_tr = 3 if gi < 2 else 2
-            if gi < n:
-                seq.append((True, 8 * s + 1 + gi, True))
-                n_tr -= 1
-            for i in range(n_tr):
-                seq.append((True, rest[r], False))
-                r += 1
-            for i in range(GT - (3 if gi < 2 else 2)):
-                seq.append((False, 4 * s + e, False))
-                e += 1
-    return seq
+def make_work():
+    work = [(False, m // GT, m % GT, False) for m in range(P1_TESTS)]
+    rest = [(False, m // GT, m % GT, False) for m in range(P1_TESTS, TEST_TILES)]
+    n_mid = len(rest) - TAIL_TESTS
+    k = 0
+    for idx in range(N_TRAIN_G):
+        on_g = idx in G_GROUPS
+        work.extend([(True, idx, i, on_g and i < G_N) for i in range(GT)])
+        if on_g and k < n_mid:
+            work.append(rest[k])
+            k += 1
+    work.extend(rest[k:])
+    return work
 
 
 def tile_rbfnet_pa_t_kernel(tc, x_train, x_test, M, out_0, out_1, out_2):
@@ -55,16 +53,17 @@ def tile_rbfnet_pa_t_kernel(tc, x_train, x_test, M, out_0, out_1, out_2):
     sm_d = out_0.rearrange("(p t) k -> p (t k)", t=TRAIN_TILES)
     sn_d = out_1.rearrange("(p t) -> p t", t=TRAIN_TILES)
     cn_d = out_2.rearrange("(p t) -> p t", t=TEST_TILES)
-    seq = make_sequence()
+    work = make_work()
+    n_work = len(work)
 
     with ExitStack() as ctx:
         keep = ctx.enter_context(tc.tile_pool(name="keep", bufs=1))
-        grp_pool = ctx.enter_context(tc.tile_pool(name="grp", bufs=3))
+        grp_pool = ctx.enter_context(tc.tile_pool(name="grp", bufs=4))
         q_pool = ctx.enter_context(tc.tile_pool(name="q", bufs=3))
-        sm_pool = ctx.enter_context(tc.tile_pool(name="smsb", bufs=8))
+        sm_pool = ctx.enter_context(tc.tile_pool(name="smsb", bufs=6))
         junk_pool = ctx.enter_context(tc.tile_pool(name="junk", bufs=2))
-        xt_pool = ctx.enter_context(tc.psum_pool(name="xtps", bufs=2))
-        ps_pool = ctx.enter_context(tc.psum_pool(name="smps", bufs=6))
+        xt_pool = ctx.enter_context(tc.psum_pool(name="xtps", bufs=3))
+        ps_pool = ctx.enter_context(tc.psum_pool(name="smps", bufs=5))
         ctx.enter_context(tc.manual_schedule())
 
         def load(src, t0, n, name):
@@ -73,38 +72,34 @@ def tile_rbfnet_pa_t_kernel(tc, x_train, x_test, M, out_0, out_1, out_2):
             return xt
 
         x_src = {}
-        m_raw = keep.tile([P, 4 * D], BF16, name="m_raw")
-        for s in range(SUPER):
+        order = []
+        m_raw = grp_pool.tile([P, 4 * D], BF16, name="grp", align_bytes=64)
+        for s in range(N_TEST_G):
+            x_src[(False, s)] = (load(xte_d, GT * s, GT, "xte%d" % s), 0)
             if s == 0:
-                a = load(xtr_d, 0, GT, "xtr0a")
                 nc.sync.dma_start(
                     out=m_raw[:].rearrange("p (u ec) -> p u ec", u=2),
                     in_=M.rearrange("(u q e) c -> q u (e c)", u=2, e=2),
                 )
-                c = load(xte_d, 0, GT, "xte0")
-                b = load(xtr_d, GT, GT, "xtr0b")
-                for i in range(GT):
-                    x_src[(True, i)] = (a, i * D)
-                    x_src[(True, GT + i)] = (b, i * D)
+                x_src[(True, 0)] = (load(xtr_d, 0, GT, "xtr0a"), 0)
+                x_src[(True, 1)] = (load(xtr_d, GT, GT, "xtr0b"), 0)
             else:
                 a = load(xtr_d, 2 * GT * s, 2 * GT, "xtr%d" % s)
-                c = load(xte_d, GT * s, GT, "xte%d" % s)
-                for i in range(2 * GT):
-                    x_src[(True, 2 * GT * s + i)] = (a, i * D)
-            for i in range(GT):
-                x_src[(False, GT * s + i)] = (c, i * D)
+                x_src[(True, 2 * s)] = (a, 0)
+                x_src[(True, 2 * s + 1)] = (a, GT * D)
+            order.extend([(False, s), (True, 2 * s), (True, 2 * s + 1)])
 
         ident = keep.tile([P, P], F32, name="ident")
         make_identity(nc, ident[:])
 
         s_norm = keep.tile([P, TRAIN_TILES], F32, name="s_norm")
         c_norm = keep.tile([P, TEST_TILES], F32, name="c_norm")
-        g_part = keep.tile([P, SUPER * G_MAX * FOLD], F32, name="g_part")
-        g_prod = keep.tile([P, G_MAX * D], F32, name="g_prod")
-        g_f1 = keep.tile([P, G_MAX * D // 2], F32, name="g_f1")
-        g_f2 = keep.tile([P, G_MAX * D // 4], F32, name="g_f2")
+        g_part = keep.tile([P, len(G_GROUPS) * G_N * FOLD], F32, name="g_part")
+        g_prod = keep.tile([P, G_N * D], F32, name="g_prod")
+        g_f1 = keep.tile([P, G_N * D // 2], F32, name="g_f1")
+        g_f2 = keep.tile([P, G_N * D // 4], F32, name="g_f2")
 
-        m_grp = keep.tile([P, 4 * D], BF16, name="m_grp", align_bytes=64)
+        m_grp = grp_pool.tile([P, 4 * D], BF16, name="grp", align_bytes=64)
         m_codes = keep.tile([P, D], U32, name="m_codes", align_bytes=64)
         m_scales = keep.tile([P, D], U8, name="m_scales", align_bytes=64)
         nc.vector.tensor_copy(
@@ -119,23 +114,18 @@ def tile_rbfnet_pa_t_kernel(tc, x_train, x_test, M, out_0, out_1, out_2):
         ps_tiles = {}
         sb_tiles = {}
         copied = {}
-        g_copied = {}
 
         def transposes(g):
+            xtile, off = x_src[order[g]]
+            x_f32 = xtile[:].bitcast(F32)
             banks = []
             for b in range(2):
                 xt = xt_pool.tile([P, 4 * P], F32, name="xt")
-                for a in range(2):
-                    is_train, t, on_g = seq[GT * g + 2 * b + a]
-                    xtile, off = x_src[(is_train, t)]
-                    x_f32 = xtile[:].bitcast(F32)
-                    for u in range(2):
-                        col = off // 2 + u * P
-                        nc.tensor.transpose(
-                            xt[:, (2 * a + u) * P : (2 * a + u + 1) * P],
-                            x_f32[:, col : col + P],
-                            ident[:],
-                        )
+                for w in range(4):
+                    col = off // 2 + (4 * b + w) * P
+                    nc.tensor.transpose(
+                        xt[:, w * P : (w + 1) * P], x_f32[:, col : col + P], ident[:]
+                    )
                 banks.append(xt)
             xt_tiles[g] = banks
 
@@ -152,15 +142,21 @@ def tile_rbfnet_pa_t_kernel(tc, x_train, x_test, M, out_0, out_1, out_2):
             grp_tiles[g] = grp
 
         def quantise(g):
-            codes = q_pool.tile([P, GT * P], U32, name="codes", align_bytes=64)
-            scales = q_pool.tile([P, GT * P], U8, name="scales", align_bytes=64)
+            is_train, gi = order[g]
+            if is_train:
+                codes = keep.tile([P, GT * P], U32, name="codes%d" % gi, align_bytes=64)
+                scales = keep.tile([P, GT * P], U8, name="scales%d" % gi, align_bytes=64)
+            else:
+                codes = q_pool.tile([P, GT * P], U32, name="codes", align_bytes=64)
+                scales = q_pool.tile([P, GT * P], U8, name="scales", align_bytes=64)
             nc.vector.quantize_mx(
                 out=codes[:].bitcast(FP8X4), scales=scales[:], in_=grp_tiles[g][:]
             )
-            q_tiles[g] = (codes, scales)
+            q_tiles[order[g]] = (codes, scales)
 
-        def mx(g, i):
-            codes, scales = q_tiles[g]
+        def mx(k):
+            is_train, gi, i, on_g = work[k]
+            codes, scales = q_tiles[(is_train, gi)]
             acc = ps_pool.tile([P, D], F32, name="acc")
             nc.tensor.matmul_mx(
                 out=acc[:],
@@ -171,109 +167,102 @@ def tile_rbfnet_pa_t_kernel(tc, x_train, x_test, M, out_0, out_1, out_2):
                 start=True,
                 stop=True,
             )
-            ps_tiles[(g, i)] = acc
+            ps_tiles[k] = acc
 
-        def halves(ap, n, width):
-            v = ap[:, : n * width].rearrange("p (n w) -> p n w", n=n)
+        def halves(ap, width):
+            v = ap[:, : G_N * width].rearrange("p (n w) -> p n w", n=G_N)
             return v[:, :, : width // 2], v[:, :, width // 2 :]
 
-        def gpsimd_batch(s):
-            n = G_TILES[s]
-            t0 = 8 * s + 1
-            xtile, off = x_src[(True, t0)]
-            sb = sb_tiles[t0 // GT]
-            col = (t0 % GT) * D
+        def gpsimd_batch(gi):
+            xtile, off = x_src[(True, gi)]
             nc.gpsimd.tensor_tensor(
-                out=g_prod[:, : n * D],
-                in0=sb[:, col : col + n * D],
-                in1=xtile[:, off : off + n * D],
+                out=g_prod[:], in0=sb_tiles[gi][:, : G_N * D], in1=xtile[:, off : off + G_N * D],
                 op=MULT,
             )
-            lo, hi = halves(g_prod, n, D)
+            lo, hi = halves(g_prod, D)
             nc.gpsimd.tensor_tensor(
-                out=g_f1[:, : n * D // 2].rearrange("p (n w) -> p n w", n=n), in0=lo, in1=hi, op=ADD
+                out=g_f1[:].rearrange("p (n w) -> p n w", n=G_N), in0=lo, in1=hi, op=ADD
             )
-            lo, hi = halves(g_f1, n, D // 2)
+            lo, hi = halves(g_f1, D // 2)
             nc.gpsimd.tensor_tensor(
-                out=g_f2[:, : n * D // 4].rearrange("p (n w) -> p n w", n=n), in0=lo, in1=hi, op=ADD
+                out=g_f2[:].rearrange("p (n w) -> p n w", n=G_N), in0=lo, in1=hi, op=ADD
             )
-            lo, hi = halves(g_f2, n, D // 4)
-            base = s * G_MAX * FOLD
+            lo, hi = halves(g_f2, D // 4)
+            base = G_GROUPS.index(gi) * G_N * FOLD
             nc.gpsimd.tensor_tensor(
-                out=g_part[:, base : base + n * FOLD].rearrange("p (n w) -> p n w", n=n),
+                out=g_part[:, base : base + G_N * FOLD].rearrange("p (n w) -> p n w", n=G_N),
                 in0=lo, in1=hi, op=ADD,
             )
 
-        def reduce_batch(s):
-            n = G_TILES[s]
-            base = s * G_MAX * FOLD
-            nc.vector.tensor_reduce(
-                out=s_norm[:, 8 * s + 1 : 8 * s + 1 + n],
-                in_=g_part[:, base : base + n * FOLD].rearrange("p (n w) -> p n w", n=n),
-                axis=mybir.AxisListType.X,
-                op=ADD,
-            )
-
-        def finish(g, i):
-            is_train, t, on_g = seq[GT * g + i]
-            xtile, off = x_src[(is_train, t)]
-            acc = ps_tiles[(g, i)]
-            x_in = xtile[:, off : off + D]
+        def finish(k, gate):
+            is_train, gi, i, on_g = work[k]
+            xtile, off = x_src[(is_train, gi)]
+            acc = ps_tiles[k]
+            x_in = xtile[:, off + i * D : off + (i + 1) * D]
+            t = gi * GT + i
             if not is_train:
-                junk = junk_pool.tile([P, D], F32, name="junk")
+                if gate:
+                    dst = g_prod[:, :D]
+                else:
+                    junk = junk_pool.tile([P, D], F32, name="junk")
+                    dst = junk[:]
                 nc.vector.scalar_tensor_tensor(
-                    out=junk[:], in0=acc[:], scalar=1.0, in1=x_in, op0=MULT, op1=MULT,
+                    out=dst, in0=acc[:], scalar=1.0, in1=x_in, op0=MULT, op1=MULT,
                     accum_out=c_norm[:, t : t + 1],
                 )
                 return
-            h = t // GT
-            if h not in sb_tiles:
-                sb_tiles[h] = sm_pool.tile([P, GT * D], F32, name="sm_sb")
-                copied[h] = 0
-            dst = sb_tiles[h][:, (t % GT) * D : (t % GT + 1) * D]
+            if gi not in sb_tiles:
+                sb_tiles[gi] = sm_pool.tile([P, GT * D], F32, name="sm_sb")
+                copied[gi] = 0
+            dst = sb_tiles[gi][:, i * D : (i + 1) * D]
             if not on_g:
                 nc.vector.scalar_tensor_tensor(
                     out=dst, in0=acc[:], scalar=1.0, in1=x_in, op0=MULT, op1=MULT,
                     accum_out=s_norm[:, t : t + 1],
                 )
             nc.scalar.copy(out=dst, in_=acc[:])
-            copied[h] += 1
-            if on_g:
-                s = t // 8
-                g_copied[s] = g_copied.get(s, 0) + 1
-                if g_copied[s] == G_TILES[s]:
-                    gpsimd_batch(s)
-            if copied[h] == GT:
-                nc.sync.dma_start(out=sm_d[:, h * GT * D : (h + 1) * GT * D], in_=sb_tiles[h][:])
+            copied[gi] += 1
+            if on_g and i == G_N - 1:
+                gpsimd_batch(gi)
+            if copied[gi] == GT:
+                nc.sync.dma_start(out=sm_d[:, gi * GT * D : (gi + 1) * GT * D], in_=sb_tiles[gi][:])
 
-        reduce_at = {}
-        late = []
-        for s in range(SUPER):
-            if G_TILES[s] > 0:
-                it = 3 * s + G_TILES[s] - 1 + R_LAG
-                if it < NG:
-                    reduce_at[it] = s
-                else:
-                    late.append(s)
+        done = 0
+        issued = 0
+        for sg in range(NL + 2):
+            if 0 <= sg - 1 < NL:
+                copy_out(sg - 1)
+            if sg < NL:
+                transposes(sg)
+            if 0 <= sg - 2 < NL:
+                quantise(sg - 2)
+            if sg >= 2 and (sg - 2) % GT == 0 and issued < P1_TESTS:
+                for i in range(GT):
+                    mx(issued)
+                    issued += 1
+            if sg >= 3:
+                finish(done, sg == NL + 1)
+                if done >= P1_TESTS - LOOK:
+                    mx(issued)
+                    issued += 1
+                done += 1
 
-        for j in range(-3, NG):
-            if 0 <= j + 2 < NG:
-                copy_out(j + 2)
-            if 0 <= j + 3 < NG:
-                transposes(j + 3)
-            has_next = 0 <= j + 1 < NG
-            if has_next:
-                quantise(j + 1)
-                mx(j + 1, 0)
-                mx(j + 1, 1)
-            if j in reduce_at:
-                reduce_batch(reduce_at[j])
-            for i in range(GT):
-                if j >= 0:
-                    finish(j, i)
-                if has_next and i < 2:
-                    mx(j + 1, i + 2)
+        def reduce_batches(q0, q1):
+            nc.vector.tensor_reduce(
+                out=s_norm[:].rearrange("p (q e) -> p q e", e=2 * GT)[:, q0:q1, :G_N],
+                in_=g_part[:].rearrange("p (q n w) -> p q n w", n=G_N, w=FOLD)[:, q0:q1],
+                axis=mybir.AxisListType.X,
+                op=ADD,
+            )
+
+        while done < n_work:
+            if work[done] == (True, R_EARLY_AT, 0, False):
+                reduce_batches(0, R_EARLY)
+            finish(done, False)
+            if issued < n_work:
+                mx(issued)
+                issued += 1
+            done += 1
         nc.sync.dma_start(out=cn_d, in_=c_norm[:])
-        for s in late:
-            reduce_batch(s)
+        reduce_batches(R_EARLY, len(G_GROUPS))
         nc.sync.dma_start(out=sn_d, in_=s_norm[:])

@@ -16,34 +16,28 @@ D = 512
 TRAIN_TILES = 64
 TEST_TILES = 32
 GT = 4
-N_TRAIN_G = TRAIN_TILES // GT
-N_TEST_G = TEST_TILES // GT
-NL = N_TRAIN_G + N_TEST_G
-P1_TESTS = 24
-TAIL_TESTS = 2
-G_GROUPS = [0, 2, 4, 6, 8, 10, 12]
+SUPER = 8
+NG = 3 * SUPER
+G_ON = [True, True, True, True, True, True, True, False]
 G_N = 2
-FOLD = 64
-LOOK = 4
-R_EARLY = 5
-R_EARLY_AT = 14
+FOLD = 128
 
 FLOPS = 2 * (TRAIN_TILES + TEST_TILES) * P * D * D
 
 
-def make_work():
-    work = [(False, m // GT, m % GT, False) for m in range(P1_TESTS)]
-    rest = [(False, m // GT, m % GT, False) for m in range(P1_TESTS, TEST_TILES)]
-    n_mid = len(rest) - TAIL_TESTS
-    k = 0
-    for idx in range(N_TRAIN_G):
-        on_g = idx in G_GROUPS
-        work.extend([(True, idx, i, on_g and i < G_N) for i in range(GT)])
-        if on_g and k < n_mid:
-            work.append(rest[k])
-            k += 1
-    work.extend(rest[k:])
-    return work
+def make_sequence():
+    seq = []
+    for s in range(SUPER):
+        tr = [(True, 8 * s + i, False) for i in range(8)]
+        te = [(False, 4 * s + i, False) for i in range(4)]
+        if s == SUPER - 1:
+            seq.extend(tr + te)
+        elif G_ON[s]:
+            seq.extend(tr[2:5] + te[0:1] + tr[5:8] + te[1:2])
+            seq.extend([(True, 8 * s, True), (True, 8 * s + 1, True)] + te[2:4])
+        else:
+            seq.extend(tr[0:3] + te[0:1] + tr[3:6] + te[1:2] + tr[6:8] + te[2:4])
+    return seq
 
 
 def tile_rbfnet_pa_t_kernel(tc, x_train, x_test, M, out_0, out_1, out_2):
@@ -53,17 +47,16 @@ def tile_rbfnet_pa_t_kernel(tc, x_train, x_test, M, out_0, out_1, out_2):
     sm_d = out_0.rearrange("(p t) k -> p (t k)", t=TRAIN_TILES)
     sn_d = out_1.rearrange("(p t) -> p t", t=TRAIN_TILES)
     cn_d = out_2.rearrange("(p t) -> p t", t=TEST_TILES)
-    work = make_work()
-    n_work = len(work)
+    seq = make_sequence()
 
     with ExitStack() as ctx:
         keep = ctx.enter_context(tc.tile_pool(name="keep", bufs=1))
-        grp_pool = ctx.enter_context(tc.tile_pool(name="grp", bufs=4))
-        q_pool = ctx.enter_context(tc.tile_pool(name="q", bufs=3))
-        sm_pool = ctx.enter_context(tc.tile_pool(name="smsb", bufs=6))
+        grp_pool = ctx.enter_context(tc.tile_pool(name="grp", bufs=5))
+        q_pool = ctx.enter_context(tc.tile_pool(name="q", bufs=4))
+        sm_pool = ctx.enter_context(tc.tile_pool(name="smsb", bufs=7))
         junk_pool = ctx.enter_context(tc.tile_pool(name="junk", bufs=2))
-        xt_pool = ctx.enter_context(tc.psum_pool(name="xtps", bufs=3))
-        ps_pool = ctx.enter_context(tc.psum_pool(name="smps", bufs=5))
+        xt_pool = ctx.enter_context(tc.psum_pool(name="xtps", bufs=2))
+        ps_pool = ctx.enter_context(tc.psum_pool(name="smps", bufs=6))
         ctx.enter_context(tc.manual_schedule())
 
         def load(src, t0, n, name):
@@ -72,34 +65,36 @@ def tile_rbfnet_pa_t_kernel(tc, x_train, x_test, M, out_0, out_1, out_2):
             return xt
 
         x_src = {}
-        order = []
-        m_raw = grp_pool.tile([P, 4 * D], BF16, name="grp", align_bytes=64)
-        for s in range(N_TEST_G):
-            x_src[(False, s)] = (load(xte_d, GT * s, GT, "xte%d" % s), 0)
+        m_raw = keep.tile([P, 4 * D], BF16, name="m_raw")
+        for s in range(SUPER):
             if s == 0:
+                a = load(xtr_d, 0, GT, "xtr0a")
                 nc.sync.dma_start(
                     out=m_raw[:].rearrange("p (u ec) -> p u ec", u=2),
                     in_=M.rearrange("(u q e) c -> q u (e c)", u=2, e=2),
                 )
-                x_src[(True, 0)] = (load(xtr_d, 0, GT, "xtr0a"), 0)
-                x_src[(True, 1)] = (load(xtr_d, GT, GT, "xtr0b"), 0)
+                c = load(xte_d, 0, GT, "xte0")
+                b = load(xtr_d, GT, GT, "xtr0b")
+                for i in range(GT):
+                    x_src[(True, i)] = (a, i * D)
+                    x_src[(True, GT + i)] = (b, i * D)
             else:
                 a = load(xtr_d, 2 * GT * s, 2 * GT, "xtr%d" % s)
-                x_src[(True, 2 * s)] = (a, 0)
-                x_src[(True, 2 * s + 1)] = (a, GT * D)
-            order.extend([(False, s), (True, 2 * s), (True, 2 * s + 1)])
+                c = load(xte_d, GT * s, GT, "xte%d" % s)
+                for i in range(2 * GT):
+                    x_src[(True, 2 * GT * s + i)] = (a, i * D)
+            for i in range(GT):
+                x_src[(False, GT * s + i)] = (c, i * D)
 
         ident = keep.tile([P, P], F32, name="ident")
         make_identity(nc, ident[:])
 
         s_norm = keep.tile([P, TRAIN_TILES], F32, name="s_norm")
         c_norm = keep.tile([P, TEST_TILES], F32, name="c_norm")
-        g_part = keep.tile([P, len(G_GROUPS) * G_N * FOLD], F32, name="g_part")
         g_prod = keep.tile([P, G_N * D], F32, name="g_prod")
         g_f1 = keep.tile([P, G_N * D // 2], F32, name="g_f1")
-        g_f2 = keep.tile([P, G_N * D // 4], F32, name="g_f2")
 
-        m_grp = grp_pool.tile([P, 4 * D], BF16, name="grp", align_bytes=64)
+        m_grp = keep.tile([P, 4 * D], BF16, name="m_grp", align_bytes=64)
         m_codes = keep.tile([P, D], U32, name="m_codes", align_bytes=64)
         m_scales = keep.tile([P, D], U8, name="m_scales", align_bytes=64)
         nc.vector.tensor_copy(
@@ -116,20 +111,28 @@ def tile_rbfnet_pa_t_kernel(tc, x_train, x_test, M, out_0, out_1, out_2):
         copied = {}
 
         def transposes(g):
-            xtile, off = x_src[order[g]]
-            x_f32 = xtile[:].bitcast(F32)
+            if g >= NG:
+                return
             banks = []
             for b in range(2):
                 xt = xt_pool.tile([P, 4 * P], F32, name="xt")
-                for w in range(4):
-                    col = off // 2 + (4 * b + w) * P
-                    nc.tensor.transpose(
-                        xt[:, w * P : (w + 1) * P], x_f32[:, col : col + P], ident[:]
-                    )
+                for a in range(2):
+                    is_train, t, on_g = seq[GT * g + 2 * b + a]
+                    xtile, off = x_src[(is_train, t)]
+                    x_f32 = xtile[:].bitcast(F32)
+                    for u in range(2):
+                        col = off // 2 + u * P
+                        nc.tensor.transpose(
+                            xt[:, (2 * a + u) * P : (2 * a + u + 1) * P],
+                            x_f32[:, col : col + P],
+                            ident[:],
+                        )
                 banks.append(xt)
             xt_tiles[g] = banks
 
         def copy_out(g):
+            if g >= NG:
+                return
             grp = grp_pool.tile([P, GT * P * 4], BF16, name="grp", align_bytes=64)
             g_f32 = grp[:].bitcast(F32)
             for b in range(2):
@@ -142,21 +145,15 @@ def tile_rbfnet_pa_t_kernel(tc, x_train, x_test, M, out_0, out_1, out_2):
             grp_tiles[g] = grp
 
         def quantise(g):
-            is_train, gi = order[g]
-            if is_train:
-                codes = keep.tile([P, GT * P], U32, name="codes%d" % gi, align_bytes=64)
-                scales = keep.tile([P, GT * P], U8, name="scales%d" % gi, align_bytes=64)
-            else:
-                codes = q_pool.tile([P, GT * P], U32, name="codes", align_bytes=64)
-                scales = q_pool.tile([P, GT * P], U8, name="scales", align_bytes=64)
+            codes = q_pool.tile([P, GT * P], U32, name="codes", align_bytes=64)
+            scales = q_pool.tile([P, GT * P], U8, name="scales", align_bytes=64)
             nc.vector.quantize_mx(
                 out=codes[:].bitcast(FP8X4), scales=scales[:], in_=grp_tiles[g][:]
             )
-            q_tiles[order[g]] = (codes, scales)
+            q_tiles[g] = (codes, scales)
 
-        def mx(k):
-            is_train, gi, i, on_g = work[k]
-            codes, scales = q_tiles[(is_train, gi)]
+        def mx(g, i):
+            codes, scales = q_tiles[g]
             acc = ps_pool.tile([P, D], F32, name="acc")
             nc.tensor.matmul_mx(
                 out=acc[:],
@@ -167,16 +164,16 @@ def tile_rbfnet_pa_t_kernel(tc, x_train, x_test, M, out_0, out_1, out_2):
                 start=True,
                 stop=True,
             )
-            ps_tiles[k] = acc
+            ps_tiles[(g, i)] = acc
 
         def halves(ap, width):
             v = ap[:, : G_N * width].rearrange("p (n w) -> p n w", n=G_N)
             return v[:, :, : width // 2], v[:, :, width // 2 :]
 
-        def gpsimd_batch(gi):
-            xtile, off = x_src[(True, gi)]
+        def gpsimd_batch(s):
+            xtile, off = x_src[(True, 8 * s)]
             nc.gpsimd.tensor_tensor(
-                out=g_prod[:], in0=sb_tiles[gi][:, : G_N * D], in1=xtile[:, off : off + G_N * D],
+                out=g_prod[:], in0=sb_tiles[2 * s][:, : G_N * D], in1=xtile[:, off : off + G_N * D],
                 op=MULT,
             )
             lo, hi = halves(g_prod, D)
@@ -185,21 +182,23 @@ def tile_rbfnet_pa_t_kernel(tc, x_train, x_test, M, out_0, out_1, out_2):
             )
             lo, hi = halves(g_f1, D // 2)
             nc.gpsimd.tensor_tensor(
-                out=g_f2[:].rearrange("p (n w) -> p n w", n=G_N), in0=lo, in1=hi, op=ADD
-            )
-            lo, hi = halves(g_f2, D // 4)
-            base = G_GROUPS.index(gi) * G_N * FOLD
-            nc.gpsimd.tensor_tensor(
-                out=g_part[:, base : base + G_N * FOLD].rearrange("p (n w) -> p n w", n=G_N),
+                out=g_prod[:, : G_N * FOLD].rearrange("p (n w) -> p n w", n=G_N),
                 in0=lo, in1=hi, op=ADD,
             )
 
-        def finish(k, gate):
-            is_train, gi, i, on_g = work[k]
-            xtile, off = x_src[(is_train, gi)]
-            acc = ps_tiles[k]
-            x_in = xtile[:, off + i * D : off + (i + 1) * D]
-            t = gi * GT + i
+        def reduce_batch(s):
+            nc.vector.tensor_reduce(
+                out=s_norm[:, 8 * s : 8 * s + G_N],
+                in_=g_prod[:, : G_N * FOLD].rearrange("p (n w) -> p n w", n=G_N),
+                axis=mybir.AxisListType.X,
+                op=ADD,
+            )
+
+        def finish(g, i, gate):
+            is_train, t, on_g = seq[GT * g + i]
+            xtile, off = x_src[(is_train, t)]
+            acc = ps_tiles[(g, i)]
+            x_in = xtile[:, off : off + D]
             if not is_train:
                 if gate:
                     dst = g_prod[:, :D]
@@ -211,58 +210,61 @@ def tile_rbfnet_pa_t_kernel(tc, x_train, x_test, M, out_0, out_1, out_2):
                     accum_out=c_norm[:, t : t + 1],
                 )
                 return
-            if gi not in sb_tiles:
-                sb_tiles[gi] = sm_pool.tile([P, GT * D], F32, name="sm_sb")
-                copied[gi] = 0
-            dst = sb_tiles[gi][:, i * D : (i + 1) * D]
+            h = t // GT
+            if h not in sb_tiles:
+                sb_tiles[h] = sm_pool.tile([P, GT * D], F32, name="sm_sb")
+                copied[h] = 0
+            dst = sb_tiles[h][:, (t % GT) * D : (t % GT + 1) * D]
             if not on_g:
                 nc.vector.scalar_tensor_tensor(
                     out=dst, in0=acc[:], scalar=1.0, in1=x_in, op0=MULT, op1=MULT,
                     accum_out=s_norm[:, t : t + 1],
                 )
             nc.scalar.copy(out=dst, in_=acc[:])
-            copied[gi] += 1
-            if on_g and i == G_N - 1:
-                gpsimd_batch(gi)
-            if copied[gi] == GT:
-                nc.sync.dma_start(out=sm_d[:, gi * GT * D : (gi + 1) * GT * D], in_=sb_tiles[gi][:])
+            copied[h] += 1
+            if copied[h] == GT:
+                nc.sync.dma_start(out=sm_d[:, h * GT * D : (h + 1) * GT * D], in_=sb_tiles[h][:])
 
-        done = 0
-        issued = 0
-        for sg in range(NL + 2):
-            if 0 <= sg - 1 < NL:
-                copy_out(sg - 1)
-            if sg < NL:
-                transposes(sg)
-            if 0 <= sg - 2 < NL:
-                quantise(sg - 2)
-            if sg >= 2 and (sg - 2) % GT == 0 and issued < P1_TESTS:
-                for i in range(GT):
-                    mx(issued)
-                    issued += 1
-            if sg >= 3:
-                finish(done, sg == NL + 1)
-                if done >= P1_TESTS - LOOK:
-                    mx(issued)
-                    issued += 1
-                done += 1
-
-        def reduce_batches(q0, q1):
-            nc.vector.tensor_reduce(
-                out=s_norm[:].rearrange("p (q e) -> p q e", e=2 * GT)[:, q0:q1, :G_N],
-                in_=g_part[:].rearrange("p (q n w) -> p q n w", n=G_N, w=FOLD)[:, q0:q1],
-                axis=mybir.AxisListType.X,
-                op=ADD,
-            )
-
-        while done < n_work:
-            if work[done] == (True, R_EARLY_AT, 0, False):
-                reduce_batches(0, R_EARLY)
-            finish(done, False)
-            if issued < n_work:
-                mx(issued)
-                issued += 1
-            done += 1
+        pending = []
+        transposes(0)
+        for j in range(-2, NG):
+            if j < 0:
+                copy_out(j + 2)
+                transposes(j + 3)
+            elif j < 2:
+                copy_out(2 * j + 2)
+                transposes(2 * j + 3)
+            else:
+                copy_out(j + 4)
+                transposes(j + 5)
+            has_next = 0 <= j + 1 < NG
+            did_r = False
+            if has_next:
+                if j + 1 < 3:
+                    quantise(j + 1)
+                elif (j + 1) % 3 == 0:
+                    for k in range(3):
+                        quantise(j + 1 + k)
+                    if len(pending) > 0:
+                        reduce_batch(pending[0])
+                        pending = pending[1:]
+                        did_r = True
+                mx(j + 1, 0)
+                mx(j + 1, 1)
+            if j == NG - 1 and len(pending) > 0:
+                reduce_batch(pending[0])
+                pending = pending[1:]
+                nc.sync.dma_start(out=sn_d, in_=s_norm[:])
+            batch = j >= 0 and j % 3 == 2 and G_ON[j // 3]
+            for i in range(GT):
+                if j >= 0:
+                    finish(j, i, batch and not did_r and i == 2)
+                if has_next and i < 2:
+                    mx(j + 1, i + 2)
+                if batch and ((did_r and i == 1) or (not did_r and i == 2)):
+                    gpsimd_batch(j // 3)
+                    pending = pending + [j // 3]
+            if 0 <= j < 2:
+                copy_out(2 * j + 3)
+                transposes(2 * j + 4)
         nc.sync.dma_start(out=cn_d, in_=c_norm[:])
-        reduce_batches(R_EARLY, len(G_GROUPS))
-        nc.sync.dma_start(out=sn_d, in_=s_norm[:])

@@ -18,9 +18,11 @@ TEST_TILES = 32
 GT = 4
 SUPER = 8
 NG = 3 * SUPER
-G_ON = [True, True, True, True, True, True, True, False]
+G_ON = [False, True, True, True, True, True, True, False]
 G_N = 2
-FOLD = 128
+FOLD = 256
+N_SINGLE = 6
+EXTRA = (1, 3)
 
 FLOPS = 2 * (TRAIN_TILES + TEST_TILES) * P * D * D
 
@@ -30,7 +32,7 @@ def make_sequence():
     for s in range(SUPER):
         tr = [(True, 8 * s + i, False) for i in range(8)]
         te = [(False, 4 * s + i, False) for i in range(4)]
-        if s == SUPER - 1:
+        if s == 0 or s == SUPER - 1:
             seq.extend(tr + te)
         elif G_ON[s]:
             seq.extend(tr[2:5] + te[0:1] + tr[5:8] + te[1:2])
@@ -73,8 +75,8 @@ def tile_rbfnet_pa_t_kernel(tc, x_train, x_test, M, out_0, out_1, out_2):
                     out=m_raw[:].rearrange("p (u ec) -> p u ec", u=2),
                     in_=M.rearrange("(u q e) c -> q u (e c)", u=2, e=2),
                 )
-                c = load(xte_d, 0, GT, "xte0")
                 b = load(xtr_d, GT, GT, "xtr0b")
+                c = load(xte_d, 0, GT, "xte0")
                 for i in range(GT):
                     x_src[(True, i)] = (a, i * D)
                     x_src[(True, GT + i)] = (b, i * D)
@@ -92,7 +94,7 @@ def tile_rbfnet_pa_t_kernel(tc, x_train, x_test, M, out_0, out_1, out_2):
         s_norm = keep.tile([P, TRAIN_TILES], F32, name="s_norm")
         c_norm = keep.tile([P, TEST_TILES], F32, name="c_norm")
         g_prod = keep.tile([P, G_N * D], F32, name="g_prod")
-        g_f1 = keep.tile([P, G_N * D // 2], F32, name="g_f1")
+        g_view = g_prod[:].rearrange("p (n w) -> p n w", n=G_N)
 
         m_grp = keep.tile([P, 4 * D], BF16, name="m_grp", align_bytes=64)
         m_codes = keep.tile([P, D], U32, name="m_codes", align_bytes=64)
@@ -166,30 +168,20 @@ def tile_rbfnet_pa_t_kernel(tc, x_train, x_test, M, out_0, out_1, out_2):
             )
             ps_tiles[(g, i)] = acc
 
-        def halves(ap, width):
-            v = ap[:, : G_N * width].rearrange("p (n w) -> p n w", n=G_N)
-            return v[:, :, : width // 2], v[:, :, width // 2 :]
-
         def gpsimd_batch(s):
             xtile, off = x_src[(True, 8 * s)]
             nc.gpsimd.tensor_tensor(
                 out=g_prod[:], in0=sb_tiles[2 * s][:, : G_N * D], in1=xtile[:, off : off + G_N * D],
                 op=MULT,
             )
-            lo, hi = halves(g_prod, D)
             nc.gpsimd.tensor_tensor(
-                out=g_f1[:].rearrange("p (n w) -> p n w", n=G_N), in0=lo, in1=hi, op=ADD
-            )
-            lo, hi = halves(g_f1, D // 2)
-            nc.gpsimd.tensor_tensor(
-                out=g_prod[:, : G_N * FOLD].rearrange("p (n w) -> p n w", n=G_N),
-                in0=lo, in1=hi, op=ADD,
+                out=g_view[:, :, :FOLD], in0=g_view[:, :, :FOLD], in1=g_view[:, :, FOLD:], op=ADD
             )
 
         def reduce_batch(s):
             nc.vector.tensor_reduce(
                 out=s_norm[:, 8 * s : 8 * s + G_N],
-                in_=g_prod[:, : G_N * FOLD].rearrange("p (n w) -> p n w", n=G_N),
+                in_=g_view[:, :, :FOLD],
                 axis=mybir.AxisListType.X,
                 op=ADD,
             )
@@ -226,21 +218,15 @@ def tile_rbfnet_pa_t_kernel(tc, x_train, x_test, M, out_0, out_1, out_2):
                 nc.sync.dma_start(out=sm_d[:, h * GT * D : (h + 1) * GT * D], in_=sb_tiles[h][:])
 
         pending = []
+        look = 2
         transposes(0)
         for j in range(-2, NG):
-            if j < 0:
-                copy_out(j + 2)
-                transposes(j + 3)
-            elif j < 2:
-                copy_out(2 * j + 2)
-                transposes(2 * j + 3)
-            else:
-                copy_out(j + 4)
-                transposes(j + 5)
+            copy_out(j + look)
+            transposes(j + look + 1)
             has_next = 0 <= j + 1 < NG
             did_r = False
             if has_next:
-                if j + 1 < 3:
+                if j + 1 < N_SINGLE:
                     quantise(j + 1)
                 elif (j + 1) % 3 == 0:
                     for k in range(3):
@@ -264,7 +250,8 @@ def tile_rbfnet_pa_t_kernel(tc, x_train, x_test, M, out_0, out_1, out_2):
                 if batch and ((did_r and i == 1) or (not did_r and i == 2)):
                     gpsimd_batch(j // 3)
                     pending = pending + [j // 3]
-            if 0 <= j < 2:
-                copy_out(2 * j + 3)
-                transposes(2 * j + 4)
+            if j in EXTRA:
+                look += 1
+                copy_out(j + look)
+                transposes(j + look + 1)
         nc.sync.dma_start(out=cn_d, in_=c_norm[:])

@@ -70,15 +70,18 @@ def tile_rbfnet_pa_t_kernel(tc, x_train, x_test, M, out_0, out_1, out_2):
         m_raw = keep.tile([P, 4 * D], BF16, name="m_raw")
         for s in range(SUPER):
             if s == 0:
-                a = load(xtr_d, 0, GT, "xtr0a")
+                a = load(xtr_d, 0, 2, "xtr0a")
                 nc.sync.dma_start(
                     out=m_raw[:].rearrange("p (u ec) -> p u ec", u=2),
                     in_=M.rearrange("(u q e) c -> q u (e c)", u=2, e=2),
                 )
+                a2 = load(xtr_d, 2, 2, "xtr0a2")
                 b = load(xtr_d, GT, GT, "xtr0b")
                 c = load(xte_d, 0, GT, "xte0")
-                for i in range(GT):
+                for i in range(2):
                     x_src[(True, i)] = (a, i * D)
+                    x_src[(True, 2 + i)] = (a2, i * D)
+                for i in range(GT):
                     x_src[(True, GT + i)] = (b, i * D)
             else:
                 a = load(xtr_d, 2 * GT * s, 2 * GT, "xtr%d" % s)
@@ -95,6 +98,8 @@ def tile_rbfnet_pa_t_kernel(tc, x_train, x_test, M, out_0, out_1, out_2):
         c_norm = keep.tile([P, TEST_TILES], F32, name="c_norm")
         g_prod = keep.tile([P, G_N * D], F32, name="g_prod")
         g_view = g_prod[:].rearrange("p (n w) -> p n w", n=G_N)
+        g_norm = keep.tile([P, SUPER], F32, name="g_norm")
+        s_junk = keep.tile([P, FOLD], F32, name="s_junk")
 
         m_grp = keep.tile([P, 4 * D], BF16, name="m_grp", align_bytes=64)
         m_codes = keep.tile([P, D], U32, name="m_codes", align_bytes=64)
@@ -180,10 +185,16 @@ def tile_rbfnet_pa_t_kernel(tc, x_train, x_test, M, out_0, out_1, out_2):
 
         def reduce_batch(s):
             nc.vector.tensor_reduce(
-                out=s_norm[:, 8 * s : 8 * s + G_N],
-                in_=g_view[:, :, :FOLD],
+                out=s_norm[:, 8 * s : 8 * s + 1],
+                in_=g_view[:, 0:1, :FOLD],
                 axis=mybir.AxisListType.X,
                 op=ADD,
+            )
+
+        def scalar_reduce(s):
+            nc.scalar.activation(
+                out=s_junk[:], in_=g_prod[:, D : D + FOLD],
+                func=mybir.ActivationFunctionType.Copy, accum_out=g_norm[:, s : s + 1],
             )
 
         def finish(g, i, gate):
@@ -221,6 +232,8 @@ def tile_rbfnet_pa_t_kernel(tc, x_train, x_test, M, out_0, out_1, out_2):
         look = 2
         transposes(0)
         for j in range(-2, NG):
+            if len(pending) > 0 and (j + 1) % 3 == 0:
+                scalar_reduce(pending[0])
             copy_out(j + look)
             transposes(j + look + 1)
             has_next = 0 <= j + 1 < NG
@@ -240,6 +253,10 @@ def tile_rbfnet_pa_t_kernel(tc, x_train, x_test, M, out_0, out_1, out_2):
             if j == NG - 1 and len(pending) > 0:
                 reduce_batch(pending[0])
                 pending = pending[1:]
+                nc.vector.tensor_copy(
+                    out=s_norm[:].rearrange("p (s e) -> p s e", e=8)[:, 1 : SUPER - 1, 1:2],
+                    in_=g_norm[:, 1 : SUPER - 1].rearrange("p (s e) -> p s e", e=1),
+                )
                 nc.sync.dma_start(out=sn_d, in_=s_norm[:])
             batch = j >= 0 and j % 3 == 2 and G_ON[j // 3]
             for i in range(GT):

@@ -20,7 +20,7 @@ SUPER = 8
 NG = 3 * SUPER
 G_ON = [False, True, True, True, True, True, True, False]
 G_N = 2
-FOLD = 256
+FOLD = 512
 N_SINGLE = 6
 EXTRA = (1, 3)
 
@@ -178,9 +178,6 @@ def tile_rbfnet_pa_t_kernel(tc, x_train, x_test, M, out_0, out_1, out_2):
             nc.gpsimd.tensor_tensor(
                 out=g_prod[:], in0=sb_tiles[2 * s][:, : G_N * D], in1=xtile[:, off : off + G_N * D],
                 op=MULT,
-            )
-            nc.gpsimd.tensor_tensor(
-                out=g_view[:, :, :FOLD], in0=g_view[:, :, :FOLD], in1=g_view[:, :, FOLD:], op=ADD
             )
 
         def reduce_batch(s):

from contextlib import ExitStack

import concourse.mybir as mybir
from concourse.masks import make_identity

FP8X4 = mybir.dt.float8_e4m3fn_x4
BF16 = mybir.dt.bfloat16
F32 = mybir.dt.float32
U32 = mybir.dt.uint32
U8 = mybir.dt.uint8
MULT = mybir.AluOpType.mult
ADD = mybir.AluOpType.add

P = 128
D = 512
TRAIN_TILES = 64
TEST_TILES = 32
GT = 4
SUPER = 8
NG = 3 * SUPER
G_ON = [False, True, True, True, True, True, True, False]
G_N = 2
FOLD = 512
N_SINGLE = 6
EXTRA = (1, 3)

FLOPS = 2 * (TRAIN_TILES + TEST_TILES) * P * D * D


def make_sequence():
    seq = []
    for s in range(SUPER):
        tr = [(True, 8 * s + i, False) for i in range(8)]
        te = [(False, 4 * s + i, False) for i in range(4)]
        if s == 0 or s == SUPER - 1:
            seq.extend(tr + te)
        elif G_ON[s]:
            seq.extend(tr[2:5] + te[0:1] + tr[5:8] + te[1:2])
            seq.extend([(True, 8 * s, True), (True, 8 * s + 1, True)] + te[2:4])
        else:
            seq.extend(tr[0:3] + te[0:1] + tr[3:6] + te[1:2] + tr[6:8] + te[2:4])
    return seq


def tile_rbfnet_pa_t_kernel(tc, x_train, x_test, M, out_0, out_1, out_2):
    nc = tc.nc
    xtr_d = x_train.rearrange("(p t) k -> p (t k)", t=TRAIN_TILES)
    xte_d = x_test.rearrange("(p t) k -> p (t k)", t=TEST_TILES)
    sm_d = out_0.rearrange("(p t) k -> p (t k)", t=TRAIN_TILES)
    sn_d = out_1.rearrange("(p t) -> p t", t=TRAIN_TILES)
    cn_d = out_2.rearrange("(p t) -> p t", t=TEST_TILES)
    seq = make_sequence()

    with ExitStack() as ctx:
        keep = ctx.enter_context(tc.tile_pool(name="keep", bufs=1))
        grp_pool = ctx.enter_context(tc.tile_pool(name="grp", bufs=5))
        q_pool = ctx.enter_context(tc.tile_pool(name="q", bufs=4))
        sm_pool = ctx.enter_context(tc.tile_pool(name="smsb", bufs=7))
        junk_pool = ctx.enter_context(tc.tile_pool(name="junk", bufs=2))
        xt_pool = ctx.enter_context(tc.psum_pool(name="xtps", bufs=2))
        ps_pool = ctx.enter_context(tc.psum_pool(name="smps", bufs=6))
        ctx.enter_context(tc.manual_schedule())

        def load(src, t0, n, name):
            xt = keep.tile([P, n * D], BF16, name=name)
            nc.sync.dma_start(out=xt[:], in_=src[:, t0 * D : (t0 + n) * D])
            return xt

        x_src = {}
        m_raw = keep.tile([P, 4 * D], BF16, name="m_raw")
        for s in range(SUPER):
            if s == 0:
                a = load(xtr_d, 0, 2, "xtr0a")
                nc.sync.dma_start(
                    out=m_raw[:].rearrange("p (u ec) -> p u ec", u=2),
                    in_=M.rearrange("(u q e) c -> q u (e c)", u=2, e=2),
                )
                a2 = load(xtr_d, 2, 2, "xtr0a2")
                b = load(xtr_d, GT, GT, "xtr0b")
                c = load(xte_d, 0, GT, "xte0")
                for i in range(2):
                    x_src[(True, i)] = (a, i * D)
                    x_src[(True, 2 + i)] = (a2, i * D)
                for i in range(GT):
                    x_src[(True, GT + i)] = (b, i * D)
            else:
                a = load(xtr_d, 2 * GT * s, 2 * GT, "xtr%d" % s)
                c = load(xte_d, GT * s, GT, "xte%d" % s)
                for i in range(2 * GT):
                    x_src[(True, 2 * GT * s + i)] = (a, i * D)
            for i in range(GT):
                x_src[(False, GT * s + i)] = (c, i * D)

        ident = keep.tile([P, P], F32, name="ident")
        make_identity(nc, ident[:])

        s_norm = keep.tile([P, TRAIN_TILES], F32, name="s_norm")
        c_norm = keep.tile([P, TEST_TILES], F32, name="c_norm")
        g_prod = keep.tile([P, G_N * D], F32, name="g_prod")
        g_view = g_prod[:].rearrange("p (n w) -> p n w", n=G_N)
        g_norm = keep.tile([P, SUPER], F32, name="g_norm")
        s_junk = keep.tile([P, FOLD], F32, name="s_junk")

        m_grp = keep.tile([P, 4 * D], BF16, name="m_grp", align_bytes=64)
        m_codes = keep.tile([P, D], U32, name="m_codes", align_bytes=64)
        m_scales = keep.tile([P, D], U8, name="m_scales", align_bytes=64)
        nc.vector.tensor_copy(
            out=m_grp[:].rearrange("p (c i t) -> p c t i", i=4, t=4),
            in_=m_raw[:].rearrange("p (t c i) -> p c t i", t=4, i=4),
        )
        nc.vector.quantize_mx(out=m_codes[:].bitcast(FP8X4), scales=m_scales[:], in_=m_grp[:])

        xt_tiles = {}
        grp_tiles = {}
        q_tiles = {}
        ps_tiles = {}
        sb_tiles = {}
        copied = {}

        def transposes(g):
            if g >= NG:
                return
            banks = []
            for b in range(2):
                xt = xt_pool.tile([P, 4 * P], F32, name="xt")
                for a in range(2):
                    is_train, t, on_g = seq[GT * g + 2 * b + a]
                    xtile, off = x_src[(is_train, t)]
                    x_f32 = xtile[:].bitcast(F32)
                    for u in range(2):
                        col = off // 2 + u * P
                        nc.tensor.transpose(
                            xt[:, (2 * a + u) * P : (2 * a + u + 1) * P],
                            x_f32[:, col : col + P],
                            ident[:],
                        )
                banks.append(xt)
            xt_tiles[g] = banks

        def copy_out(g):
            if g >= NG:
                return
            grp = grp_pool.tile([P, GT * P * 4], BF16, name="grp", align_bytes=64)
            g_f32 = grp[:].bitcast(F32)
            for b in range(2):
                nc.scalar.copy(
                    out=g_f32[:, 4 * P * b : 4 * P * (b + 1)].rearrange(
                        "p (a r u) -> p a r u", a=2, u=2
                    ),
                    in_=xt_tiles[g][b][:].rearrange("p (a u r) -> p a r u", a=2, u=2),
                )
            grp_tiles[g] = grp

        def quantise(g):
            codes = q_pool.tile([P, GT * P], U32, name="codes", align_bytes=64)
            scales = q_pool.tile([P, GT * P], U8, name="scales", align_bytes=64)
            nc.vector.quantize_mx(
                out=codes[:].bitcast(FP8X4), scales=scales[:], in_=grp_tiles[g][:]
            )
            q_tiles[g] = (codes, scales)

        def mx(g, i):
            codes, scales = q_tiles[g]
            acc = ps_pool.tile([P, D], F32, name="acc")
            nc.tensor.matmul_mx(
                out=acc[:],
                lhsT=codes[:, i * P : (i + 1) * P].bitcast(FP8X4),
                lhsT_scale=scales[:, i * P : (i + 1) * P],
                rhs=m_codes[:].bitcast(FP8X4),
                rhs_scale=m_scales[:],
                start=True,
                stop=True,
            )
            ps_tiles[(g, i)] = acc

        def gpsimd_batch(s):
            xtile, off = x_src[(True, 8 * s)]
            nc.gpsimd.tensor_tensor(
                out=g_prod[:], in0=sb_tiles[2 * s][:, : G_N * D], in1=xtile[:, off : off + G_N * D],
                op=MULT,
            )

        def reduce_batch(s):
            nc.vector.tensor_reduce(
                out=s_norm[:, 8 * s : 8 * s + 1],
                in_=g_view[:, 0:1, :FOLD],
                axis=mybir.AxisListType.X,
                op=ADD,
            )

        def scalar_reduce(s):
            nc.scalar.activation(
                out=s_junk[:], in_=g_prod[:, D : D + FOLD],
                func=mybir.ActivationFunctionType.Copy, accum_out=g_norm[:, s : s + 1],
            )

        def finish(g, i, gate):
            is_train, t, on_g = seq[GT * g + i]
            xtile, off = x_src[(is_train, t)]
            acc = ps_tiles[(g, i)]
            x_in = xtile[:, off : off + D]
            if not is_train:
                if gate:
                    dst = g_prod[:, :D]
                else:
                    junk = junk_pool.tile([P, D], F32, name="junk")
                    dst = junk[:]
                nc.vector.scalar_tensor_tensor(
                    out=dst, in0=acc[:], scalar=1.0, in1=x_in, op0=MULT, op1=MULT,
                    accum_out=c_norm[:, t : t + 1],
                )
                return
            h = t // GT
            if h not in sb_tiles:
                sb_tiles[h] = sm_pool.tile([P, GT * D], F32, name="sm_sb")
                copied[h] = 0
            dst = sb_tiles[h][:, (t % GT) * D : (t % GT + 1) * D]
            if not on_g:
                nc.vector.scalar_tensor_tensor(
                    out=dst, in0=acc[:], scalar=1.0, in1=x_in, op0=MULT, op1=MULT,
                    accum_out=s_norm[:, t : t + 1],
                )
            nc.scalar.copy(out=dst, in_=acc[:])
            copied[h] += 1
            if copied[h] == GT:
                nc.sync.dma_start(out=sm_d[:, h * GT * D : (h + 1) * GT * D], in_=sb_tiles[h][:])

        pending = []
        look = 2
        transposes(0)
        for j in range(-2, NG):
            if len(pending) > 0 and (j + 1) % 3 == 0:
                scalar_reduce(pending[0])
            copy_out(j + look)
            transposes(j + look + 1)
            has_next = 0 <= j + 1 < NG
            did_r = False
            if has_next:
                if j + 1 < N_SINGLE:
                    quantise(j + 1)
                elif (j + 1) % 3 == 0:
                    for k in range(3):
                        quantise(j + 1 + k)
                    if len(pending) > 0:
                        reduce_batch(pending[0])
                        pending = pending[1:]
                        did_r = True
                mx(j + 1, 0)
                mx(j + 1, 1)
            if j == NG - 1 and len(pending) > 0:
                reduce_batch(pending[0])
                pending = pending[1:]
                nc.vector.tensor_copy(
                    out=s_norm[:].rearrange("p (s e) -> p s e", e=8)[:, 1 : SUPER - 1, 1:2],
                    in_=g_norm[:, 1 : SUPER - 1].rearrange("p (s e) -> p s e", e=1),
                )
                nc.sync.dma_start(out=sn_d, in_=s_norm[:])
            batch = j >= 0 and j % 3 == 2 and G_ON[j // 3]
            for i in range(GT):
                if j >= 0:
                    finish(j, i, batch and not did_r and i == 2)
                if has_next and i < 2:
                    mx(j + 1, i + 2)
                if batch and ((did_r and i == 1) or (not did_r and i == 2)):
                    gpsimd_batch(j // 3)
                    pending = pending + [j // 3]
            if j in EXTRA:
                look += 1
                copy_out(j + look)
                transposes(j + look + 1)
        nc.sync.dma_start(out=cn_d, in_=c_norm[:])
